import numpy as np
import ml_dtypes


def mxq(x, axis, fmt="e4m3"):
    dtype, down = {"e4m3": (ml_dtypes.float8_e4m3fn, 7), "e5m2": (ml_dtypes.float8_e5m2, 14)}[fmt]
    v = np.moveaxis(np.asarray(x, np.float32).astype(ml_dtypes.bfloat16).astype(np.float64), axis, -1)
    blocks = v.reshape(v.shape[:-1] + (-1, 32))
    amax = np.abs(blocks).max(-1, keepdims=True)
    byte = np.maximum(np.where(amax > 0, np.frexp(amax)[1] - 1 + 127, 0) - down, 1)
    scale = np.exp2(byte - 127.0)
    codes = (blocks / scale).astype(np.float32).astype(dtype).astype(np.float64)
    return np.moveaxis((codes * scale).reshape(v.shape), -1, axis)


WIDE = False


def mx_kscale(k):
    if not WIDE:
        return np.ones(k)
    levels = np.array([10, -10, 5, -5, 0])
    a = np.random.permutation(np.resize(levels, k // 512 * 4)).reshape(k // 512, 4)
    idx = np.arange(k)
    return np.exp2(a[idx // 512, idx % 128 // 32])


BF16 = ml_dtypes.bfloat16


def bf(x):
    return np.asarray(x, np.float32).astype(BF16)


def f64(x):
    return np.asarray(x).astype(np.float64)


E2M1 = np.array([0.0, 0.5, 1.0, 1.5, 2.0, 3.0, 4.0, 6.0, -0.0, -0.5, -1.0, -1.5, -2.0, -3.0, -4.0, -6.0])


def pack_weight(w, fmt):
    k, n = w.shape
    w = f64(bf(w)).reshape(k // 32, 32, n)
    amax = np.abs(w).max(1)
    if fmt == "e4m3":
        byte = np.frexp(amax)[1] - 1 + 127 - 7
    else:
        mant, ex = np.frexp(amax / 6.0)
        byte = np.where(mant > 0.5, ex, ex - 1) + 127
    byte = np.clip(np.where(amax > 0, byte, 1), 1, 254)
    scaled = (w * np.exp2(127.0 - byte)[:, None, :]).reshape(k, n).astype(np.float32)
    by_word = np.ascontiguousarray(scaled.reshape(k // 512, 128, 4, n).transpose(0, 1, 3, 2))
    if fmt == "e4m3":
        words = by_word.astype(ml_dtypes.float8_e4m3fn).view(np.uint8)
    else:
        c = by_word.astype(ml_dtypes.float4_e2m1fn).view(np.uint8) & 0xF
        words = c[..., 0::2] | (c[..., 1::2] << 4)
    return np.ascontiguousarray(words), np.ascontiguousarray(byte.astype(np.uint8).reshape(k // 512, 16, n))


def unpack_weight(words, scales, fmt):
    g, p, n, _ = words.shape
    if fmt == "e4m3":
        vals = np.ascontiguousarray(words).view(ml_dtypes.float8_e4m3fn).astype(np.float64)
    else:
        nib = np.empty((g, p, n, 4), np.uint8)
        nib[..., 0::2] = words & 0xF
        nib[..., 1::2] = words >> 4
        vals = E2M1[nib]
    vals = vals * np.repeat(np.exp2(scales.astype(np.float64) - 127.0), 8, axis=1)[..., None]
    return vals.transpose(0, 1, 3, 2).reshape(g * 512, n)

def pack4(w):
    words, scales = pack_weight(w, "e2m1")
    return words.reshape(words.shape[0], 128, -1), scales


def unpack4(words, scales):
    return unpack_weight(words.reshape(words.shape[0], 128, -1, 2), scales, "e2m1")


B, I, H = 1024, 512, 512


def sigmoid(v):
    return 1.0 / (1.0 + np.exp(-v))


def setup_inputs():
    s = mx_kscale(I)
    x = bf(np.random.standard_normal((B, I)) * s)
    h_prev = bf(np.random.standard_normal((B, H)))
    c_prev = bf(np.random.standard_normal((B, H)))
    w_ih = np.random.standard_normal((4 * H, I)) * 1.0 / np.sqrt(I) / s[None, :]
    w_ih_words, w_ih_scales = pack4(np.ascontiguousarray(w_ih.T))
    w_hh = bf(np.random.standard_normal((4 * H, H)) * 1.0 / np.sqrt(H))
    bias_ih = bf(np.random.standard_normal(4 * H) * 0.5)
    bias_hh = bf(np.random.standard_normal(4 * H) * 0.5)
    return {"x": x,
            "h_prev": h_prev,
            "c_prev": c_prev,
            "w_ih_words": w_ih_words,
            "w_ih_scales": w_ih_scales,
            "w_hh": w_hh,
            "bias_ih": bias_ih,
            "bias_hh": bias_hh}


def reference(x, h_prev, c_prev, w_ih_words, w_ih_scales, w_hh, bias_ih, bias_hh):
    gates = (mxq(f64(x), 1, "e4m3") @ unpack4(w_ih_words, w_ih_scales)) + f64(bias_ih) + f64(h_prev) @ f64(w_hh).T + f64(bias_hh)
    i_g, f_g, g_g, o_g = np.split(gates, 4, axis=1)
    i_g = sigmoid(i_g)
    f_g = sigmoid(f_g)
    g_g = np.tanh(g_g)
    o_g = sigmoid(o_g)
    c_new = f_g * f64(c_prev) + i_g * g_g
    h_new = o_g * np.tanh(c_new)
    return (h_new, c_new)

@@ -1,0 +1,312 @@
+from contextlib import ExitStack
+
+import concourse.mybir as mybir
+from concourse.masks import make_identity
+
+F32 = mybir.dt.float32
+BF16 = mybir.dt.bfloat16
+I32 = mybir.dt.int32
+U32 = mybir.dt.uint32
+U8 = mybir.dt.uint8
+FP8X4 = mybir.dt.float8_e4m3fn_x4
+FP4X4 = mybir.dt.float4_e2m1fn_x4
+ADD = mybir.AluOpType.add
+MULT = mybir.AluOpType.mult
+SIGMOID = mybir.ActivationFunctionType.Sigmoid
+TANH = mybir.ActivationFunctionType.Tanh
+
+P = 128
+BATCH, IN, HID = 1024, 512, 512
+GATES = 4
+TILES = BATCH // P
+PAIRS = TILES // 2
+BANK = 512
+PSUM_BANKS = 8
+HALVES = 2
+WORD = 2
+ROWS = HID // P
+
+I_GATE, F_GATE, G_GATE, O_GATE = 0, 1, 2, 3
+GATE_ORDER = (I_GATE, G_GATE, F_GATE, O_GATE)
+GATE_FUNC = (SIGMOID, SIGMOID, TANH, SIGMOID)
+
+LEAD = 2
+HEAD_LEAD = 2
+
+HEAD_PAIRS = 2
+assert 2 * HEAD_PAIRS >= LEAD + 1
+
+FLOPS = 2 * BATCH * GATES * HID * (IN + HID)
+
+
+def tile_int8lstmcell_kernel(
+    tc, x, h_prev, c_prev, w_ih_words, w_ih_scales, w_hh, bias_ih, bias_hh, out_0, out_1
+):
+    nc = tc.nc
+    with ExitStack() as ctx:
+        ctx.enter_context(tc.manual_schedule())
+        keep = ctx.enter_context(tc.tile_pool(name="keep", bufs=1))
+        ahead = ctx.enter_context(tc.tile_pool(name="ahead", bufs=LEAD + 2))
+        work = ctx.enter_context(tc.tile_pool(name="work", bufs=3))
+        psum = ctx.enter_context(tc.psum_pool(name="psum", bufs=PSUM_BANKS))
+
+        x_rows = x.rearrange("(p t) k -> p t k", t=TILES)
+        h_rows = h_prev.rearrange("(p t) k -> p t k", t=TILES)
+        c_rows = c_prev.rearrange("(p t) n -> p t n", t=TILES)
+        h_out = out_0.rearrange("(p t) n -> p t n", t=TILES)
+        c_out = out_1.rearrange("(p t) n -> p t n", t=TILES)
+        w_rows = w_hh.rearrange("(q p r) k -> q p (r k)", q=GATES, r=ROWS)
+
+        bias_rows = keep.tile([P, GATES * HID], BF16, name="bias_rows")
+        nc.vector.memset(bias_rows[:].bitcast(I32), 0)
+        ones = keep.tile([P, P], BF16, name="ones")
+        nc.vector.memset(ones[:], 1.0)
+        w_scales = keep.tile([P, GATES * HID], U8, name="w_scales", align_bytes=64)
+        nc.vector.memset(w_scales[:].bitcast(I32), 0)
+        ident = keep.tile([P, P], F32, name="ident")
+        make_identity(nc, ident[:])
+        warm = keep.tile([P, 1], F32, name="warm")
+        nc.vector.memset(warm[:], 0.0)
+        nc.scalar.activation(out=warm[:], in_=warm[:], func=SIGMOID)
+
+        x_raw = keep.tile([P, TILES, IN], BF16, name="x_raw")
+        w_codes = keep.tile([P, 2 * GATES * HID], U8, name="w_codes", align_bytes=64)
+
+        def load_x_pair(j):
+            nc.sync.dma_start(out=x_raw[:, 2 * j : 2 * j + 2, :], in_=x_rows[:, 2 * j : 2 * j + 2, :])
+
+        load_x_pair(0)
+        load_x_pair(1)
+        nc.sync.dma_start(out=bias_rows[0:1, :], in_=bias_ih.unsqueeze(0))
+        nc.sync.dma_start(out=bias_rows[1:2, :], in_=bias_hh.unsqueeze(0))
+        nc.sync.dma_start(out=w_codes[:].bitcast(I32), in_=w_ih_words[0].bitcast(I32))
+        for quadrant in range(4):
+            nc.sync.dma_start(
+                out=w_scales[32 * quadrant : 32 * quadrant + 4, :].bitcast(I32),
+                in_=w_ih_scales[0, 4 * quadrant : 4 * quadrant + 4, :].bitcast(I32),
+            )
+        w_raw = keep.tile([P, GATES, ROWS * HID], BF16, name="w_raw")
+        h_raw = keep.tile([P, TILES, HID], BF16, name="h_raw")
+
+        def load_h_pair(j):
+            nc.sync.dma_start(out=h_raw[:, 2 * j : 2 * j + 2, :], in_=h_rows[:, 2 * j : 2 * j + 2, :])
+
+        for step, q in enumerate(GATE_ORDER):
+            nc.sync.dma_start(out=w_raw[:, q, :], in_=w_rows[q])
+            if step == 0:
+                load_h_pair(0)
+        for j in range(HEAD_PAIRS, PAIRS):
+            load_x_pair(j)
+        for j in range(1, PAIRS):
+            load_h_pair(j)
+        c_raw = keep.tile([P, TILES, HID], BF16, name="c_raw")
+        nc.sync.dma_start(out=c_raw[:], in_=c_rows)
+
+        bias_sum = keep.tile([P, GATES, HID], F32, name="bias_sum")
+        x_words = x_raw[:].bitcast(F32)
+        grouped = keep.tile([P, TILES * IN], BF16, name="grouped", align_bytes=64)
+        grouped_words = grouped[:].bitcast(F32).rearrange("p (t b u) -> p t b u", t=TILES, u=HALVES)
+        x_codes = keep.tile([P, BATCH], U32, name="x_codes", align_bytes=64)
+        x_scales = keep.tile([P, BATCH], U8, name="x_scales", align_bytes=64)
+
+        open_banks = {}
+
+        def turn_x_step(j, k):
+            if k == 0:
+                open_banks["x", j] = psum.tile([P, BANK], F32, name="bank")
+            planes = open_banks["x", j][:].rearrange("p (t u b) -> p t u b", t=2, u=HALVES)
+            i, u = divmod(k, HALVES)
+            nc.tensor.transpose(
+                out=planes[:, i, u, :],
+                in_=x_words[:, 2 * j + i, u : IN // WORD : HALVES],
+                identity=ident[:],
+            )
+            if k == 2 * HALVES - 1:
+                nc.scalar.copy(
+                    out=grouped_words[:, 2 * j : 2 * j + 2, :, :],
+                    in_=planes.rearrange("p t u b -> p t b u"),
+                )
+
+        def turn_x_pair(j):
+            for k in range(2 * HALVES):
+                turn_x_step(j, k)
+
+        def quantise_x_pair(j):
+            rows = slice(2 * j * P, (2 * j + 2) * P)
+            nc.vector.quantize_mx(
+                out=x_codes[:, rows].bitcast(FP8X4),
+                scales=x_scales[:, rows],
+                in_=grouped[:, 2 * j * IN : (2 * j + 2) * IN],
+            )
+
+        def spread_bias(q):
+            bank = psum.tile([P, BANK], F32, name="bank")
+            nc.tensor.matmul(
+                out=bank[:], lhsT=ones[:], rhs=bias_rows[:, q * HID : (q + 1) * HID], start=True, stop=True
+            )
+            nc.scalar.copy(out=bias_sum[:, q, :], in_=bank[:])
+
+        for j in range(HEAD_PAIRS):
+            turn_x_pair(j)
+            quantise_x_pair(j)
+            for q in GATE_ORDER[j * GATES // HEAD_PAIRS : (j + 1) * GATES // HEAD_PAIRS]:
+                spread_bias(q)
+
+        from_x = {}
+
+        def input_product(t, q):
+            if t not in from_x:
+                from_x[t] = ahead.tile([P, GATES, HID], F32, name="from_x")
+            bank = psum.tile([P, BANK], F32, name="bank")
+            nc.tensor.matmul_mx(
+                out=bank[:],
+                lhsT=x_codes[:, t * P : (t + 1) * P].bitcast(FP8X4),
+                lhsT_scale=x_scales[:, t * P : (t + 1) * P],
+                rhs=w_codes[:, 2 * q * HID : 2 * (q + 1) * HID].bitcast(FP4X4),
+                rhs_scale=w_scales[:, q * HID : (q + 1) * HID],
+                start=True,
+                stop=True,
+            )
+            nc.vector.tensor_tensor(out=from_x[t][:, q, :], in0=bank[:], in1=bias_sum[:, q, :], op=ADD)
+
+        w_words = w_raw[:].bitcast(F32)
+        h_words = h_raw[:].bitcast(F32)
+        wT_words = keep.tile([P, HALVES, GATES, HID], F32, name="wT_words")
+        hT_words = keep.tile([P, HALVES, TILES, P], F32, name="hT_words")
+
+        def turn_h_step(j, k):
+            if k == 0:
+                open_banks["h", j] = psum.tile([P, BANK], F32, name="bank")
+            planes = open_banks["h", j][:].rearrange("p (u t b) -> p u t b", u=HALVES, t=2)
+            u, i = divmod(k, 2)
+            nc.tensor.transpose(
+                out=planes[:, u, i, :],
+                in_=h_words[:, 2 * j + i, u * P : (u + 1) * P],
+                identity=ident[:],
+            )
+            if k == 2 * HALVES - 1:
+                nc.scalar.copy(out=hT_words[:, :, 2 * j : 2 * j + 2, :], in_=planes)
+
+        def turn_h_pair(j):
+            for k in range(2 * HALVES):
+                turn_h_step(j, k)
+
+        def turn_w_step(block, k):
+            u, r = divmod(k, ROWS)
+            if r == 0:
+                open_banks["w", block] = psum.tile([P, BANK], F32, name="bank")
+            bank = open_banks["w", block]
+            first = r * (HID // WORD) + u * P
+            nc.tensor.transpose(
+                out=bank[:, r * P : (r + 1) * P],
+                in_=w_words[:, block, first : first + P],
+                identity=ident[:],
+            )
+            if r == ROWS - 1:
+                nc.scalar.copy(
+                    out=wT_words[:, u, block, :].rearrange("p (n r) -> p n r", r=ROWS),
+                    in_=bank[:].rearrange("p (r n) -> p n r", r=ROWS),
+                )
+
+        for step in range(HEAD_LEAD):
+            for q in GATE_ORDER:
+                input_product(step, q)
+            if step == 0:
+                for k in range(HALVES * ROWS):
+                    turn_w_step(GATE_ORDER[0], k)
+                turn_h_pair(0)
+        woven = [(turn_w_step, block, k) for block in GATE_ORDER[1:] for k in range(HALVES * ROWS)]
+        DOUBLE = len(woven)
+        woven.extend([(turn_x_step, j, k) for j in range(HEAD_PAIRS, PAIRS) for k in range(2 * HALVES)])
+        woven.extend([(turn_h_step, j, k) for j in range(1, PAIRS) for k in range(2 * HALVES)])
+        woven_done = [0]
+
+        wT = wT_words[:].bitcast(BF16).rearrange("p u q (n e) -> p u q n e", e=WORD)
+        hT = hT_words[:].bitcast(BF16).rearrange("p u t (b e) -> p u t b e", e=WORD)
+
+        acts = {}
+        cells = {}
+        kept = {}
+        tanhs = {}
+
+        def gate(t, q):
+            if t == 0:
+                for late in range(HEAD_LEAD, LEAD):
+                    input_product(late, q)
+            if t + LEAD < TILES:
+                input_product(t + LEAD, q)
+            if t not in acts:
+                acts[t] = work.tile([P, GATES, HID], F32, name="acts")
+            bank = psum.tile([P, BANK], F32, name="bank")
+            for u in range(HALVES):
+                for e in range(WORD):
+                    nc.tensor.matmul(
+                        out=bank[:],
+                        lhsT=hT[:, u, t, :, e],
+                        rhs=wT[:, u, q, :, e],
+                        start=(u == 0 and e == 0),
+                        stop=(u == HALVES - 1 and e == WORD - 1),
+                    )
+                    for again in range(2 if woven_done[0] < DOUBLE else 1):
+                        if woven_done[0] < len(woven):
+                            step, j, k = woven[woven_done[0]]
+                            woven_done[0] += 1
+                            step(j, k)
+            pre = work.tile([P, HID], F32, name="pre")
+            nc.vector.tensor_tensor(out=pre[:], in0=bank[:], in1=from_x[t][:, q, :], op=ADD)
+            nc.scalar.activation(out=acts[t][:, q, :], in_=pre[:], func=GATE_FUNC[q])
+
+        def input_term(t, engine):
+            cells[t] = work.tile([P, HID], F32, name="c_new")
+            engine.tensor_tensor(out=cells[t][:], in0=acts[t][:, I_GATE, :], in1=acts[t][:, G_GATE, :], op=MULT)
+
+        def forget_term(t, engine):
+            kept[t] = work.tile([P, HID], F32, name="fc")
+            engine.tensor_tensor(out=kept[t][:], in0=acts[t][:, F_GATE, :], in1=c_raw[:, t, :], op=MULT)
+
+        def cell_state(t, engine):
+            engine.tensor_tensor(out=cells[t][:], in0=cells[t][:], in1=kept[t][:], op=ADD)
+            nc.sync.dma_start(out=c_out[:, t, :], in_=cells[t][:])
+
+        def cell_tanh(t):
+            tanhs[t] = work.tile([P, HID], F32, name="tanh_c")
+            nc.scalar.activation(out=tanhs[t][:], in_=cells[t][:], func=TANH)
+
+        def hidden_state(t, engine):
+            h_new = work.tile([P, HID], F32, name="h_new")
+            engine.tensor_tensor(out=h_new[:], in0=acts[t][:, O_GATE, :], in1=tanhs[t][:], op=MULT)
+            nc.sync.dma_start(out=h_out[:, t, :], in_=h_new[:])
+
+        LAST = TILES - 1
+        for t in range(TILES):
+            busy = t < LAST
+            was_busy = True
+            if t != 1:
+                gate(t, I_GATE)
+            if t == 0:
+                gate(1, I_GATE)
+            gate(t, G_GATE)
+            if not was_busy:
+                cell_state(t - 1, nc.vector)
+                cell_tanh(t - 1)
+            gate(t, F_GATE)
+            input_term(t, nc.vector if t == LAST else nc.gpsimd)
+            if t > 0 and was_busy:
+                cell_tanh(t - 1)
+            if t < LAST - 1:
+                gate(t, O_GATE)
+            if t == LAST:
+                gate(t - 1, O_GATE)
+            if t == 0:
+                for j in range(HEAD_PAIRS, PAIRS):
+                    quantise_x_pair(j)
+            forget_term(t, nc.vector if t == LAST else nc.gpsimd)
+            if busy:
+                cell_state(t, nc.gpsimd)
+            if t == LAST:
+                gate(t, O_GATE)
+                cell_state(t, nc.vector)
+            if t > 0:
+                hidden_state(t - 1, nc.gpsimd if busy else nc.vector)
+        cell_tanh(LAST)
+        hidden_state(LAST, nc.vector)

@@ -46,8 +46,7 @@ def tile_int8lstmcell_kernel(
     with ExitStack() as ctx:
         ctx.enter_context(tc.manual_schedule())
         keep = ctx.enter_context(tc.tile_pool(name="keep", bufs=1))
-        ahead = ctx.enter_context(tc.tile_pool(name="ahead", bufs=LEAD + 2))
-        work = ctx.enter_context(tc.tile_pool(name="work", bufs=3))
+        states = ctx.enter_context(tc.tile_pool(name="states", bufs=TILES))
         psum = ctx.enter_context(tc.psum_pool(name="psum", bufs=PSUM_BANKS))
 
         x_rows = x.rearrange("(p t) k -> p t k", t=TILES)
@@ -152,11 +151,9 @@ def tile_int8lstmcell_kernel(
             for q in GATE_ORDER[j * GATES // HEAD_PAIRS : (j + 1) * GATES // HEAD_PAIRS]:
                 spread_bias(q)
 
-        from_x = {}
+        gates = [states.tile([P, GATES, HID], F32, name="gates") for t in range(TILES)]
 
         def input_product(t, q):
-            if t not in from_x:
-                from_x[t] = ahead.tile([P, GATES, HID], F32, name="from_x")
             bank = psum.tile([P, BANK], F32, name="bank")
             nc.tensor.matmul_mx(
                 out=bank[:],
@@ -167,7 +164,7 @@ def tile_int8lstmcell_kernel(
                 start=True,
                 stop=True,
             )
-            nc.vector.tensor_tensor(out=from_x[t][:, q, :], in0=bank[:], in1=bias_sum[:, q, :], op=ADD)
+            nc.vector.tensor_tensor(out=gates[t][:, q, :], in0=bank[:], in1=bias_sum[:, q, :], op=ADD)
 
         w_words = w_raw[:].bitcast(F32)
         h_words = h_raw[:].bitcast(F32)
@@ -224,19 +221,12 @@ def tile_int8lstmcell_kernel(
         wT = wT_words[:].bitcast(BF16).rearrange("p u q (n e) -> p u q n e", e=WORD)
         hT = hT_words[:].bitcast(BF16).rearrange("p u t (b e) -> p u t b e", e=WORD)
 
-        acts = {}
-        cells = {}
-        kept = {}
-        tanhs = {}
-
         def gate(t, q):
             if t == 0:
                 for late in range(HEAD_LEAD, LEAD):
                     input_product(late, q)
             if t + LEAD < TILES:
                 input_product(t + LEAD, q)
-            if t not in acts:
-                acts[t] = work.tile([P, GATES, HID], F32, name="acts")
             bank = psum.tile([P, BANK], F32, name="bank")
             for u in range(HALVES):
                 for e in range(WORD):
@@ -252,30 +242,30 @@ def tile_int8lstmcell_kernel(
                             step, j, k = woven[woven_done[0]]
                             woven_done[0] += 1
                             step(j, k)
-            pre = work.tile([P, HID], F32, name="pre")
-            nc.vector.tensor_tensor(out=pre[:], in0=bank[:], in1=from_x[t][:, q, :], op=ADD)
-            nc.scalar.activation(out=acts[t][:, q, :], in_=pre[:], func=GATE_FUNC[q])
+            value = gates[t][:, q, :]
+            nc.vector.tensor_tensor(out=value, in0=bank[:], in1=value, op=ADD)
+            nc.scalar.activation(out=value, in_=value, func=GATE_FUNC[q])
 
         def input_term(t, engine):
-            cells[t] = work.tile([P, HID], F32, name="c_new")
-            engine.tensor_tensor(out=cells[t][:], in0=acts[t][:, I_GATE, :], in1=acts[t][:, G_GATE, :], op=MULT)
+            i, g = gates[t][:, I_GATE, :], gates[t][:, G_GATE, :]
+            engine.tensor_tensor(out=i, in0=i, in1=g, op=MULT)
 
         def forget_term(t, engine):
-            kept[t] = work.tile([P, HID], F32, name="fc")
-            engine.tensor_tensor(out=kept[t][:], in0=acts[t][:, F_GATE, :], in1=c_raw[:, t, :], op=MULT)
+            f = gates[t][:, F_GATE, :]
+            engine.tensor_tensor(out=f, in0=f, in1=c_raw[:, t, :], op=MULT)
 
         def cell_state(t, engine):
-            engine.tensor_tensor(out=cells[t][:], in0=cells[t][:], in1=kept[t][:], op=ADD)
-            nc.sync.dma_start(out=c_out[:, t, :], in_=cells[t][:])
+            i, f = gates[t][:, I_GATE, :], gates[t][:, F_GATE, :]
+            engine.tensor_tensor(out=f, in0=i, in1=f, op=ADD)
+            nc.sync.dma_start(out=c_out[:, t, :], in_=f)
 
         def cell_tanh(t):
-            tanhs[t] = work.tile([P, HID], F32, name="tanh_c")
-            nc.scalar.activation(out=tanhs[t][:], in_=cells[t][:], func=TANH)
+            nc.scalar.activation(out=gates[t][:, G_GATE, :], in_=gates[t][:, F_GATE, :], func=TANH)
 
         def hidden_state(t, engine):
-            h_new = work.tile([P, HID], F32, name="h_new")
-            engine.tensor_tensor(out=h_new[:], in0=acts[t][:, O_GATE, :], in1=tanhs[t][:], op=MULT)
-            nc.sync.dma_start(out=h_out[:, t, :], in_=h_new[:])
+            g, o = gates[t][:, G_GATE, :], gates[t][:, O_GATE, :]
+            engine.tensor_tensor(out=o, in0=o, in1=g, op=MULT)
+            nc.sync.dma_start(out=h_out[:, t, :], in_=o)
 
         LAST = TILES - 1
         for t in range(TILES):

@@ -30,11 +30,23 @@ I_GATE, F_GATE, G_GATE, O_GATE = 0, 1, 2, 3
 GATE_ORDER = (I_GATE, G_GATE, F_GATE, O_GATE)
 GATE_FUNC = (SIGMOID, SIGMOID, TANH, SIGMOID)
 
-LEAD = 2
-HEAD_LEAD = 2
+LAST = TILES - 1
+UNITS = (
+    [(0, I_GATE), (1, I_GATE), (0, G_GATE), (0, F_GATE), (0, O_GATE), (1, G_GATE), (1, F_GATE), (1, O_GATE)]
+    + [(t, q) for t in range(2, LAST - 2) for q in GATE_ORDER]
+    + [(t, q) for t in (LAST - 2, LAST - 1, LAST) for q in GATE_ORDER[:3]]
+    + [(t, O_GATE) for t in (LAST - 2, LAST - 1, LAST)]
+)
 
-HEAD_PAIRS = 2
-assert 2 * HEAD_PAIRS >= LEAD + 1
+
+def x_products_before(i):
+    return min(3 + 5 * i // 4, i + 8, len(UNITS))
+
+
+WEAVE = ((2, 2, 2, 2), (1, 1, 1, 1))
+HASTY = 3
+QUANTISE_BEHIND = {3: 1, 8: 2, 12: 3}
+TANH_BEHIND = 4
 
 FLOPS = 2 * BATCH * GATES * HID * (IN + HID)
 
@@ -70,36 +82,38 @@ def tile_int8lstmcell_kernel(
 
         x_raw = keep.tile([P, TILES, IN], BF16, name="x_raw")
         w_codes = keep.tile([P, 2 * GATES * HID], U8, name="w_codes", align_bytes=64)
+        w_raw = keep.tile([P, GATES, ROWS * HID], BF16, name="w_raw")
+        h_raw = keep.tile([P, TILES, HID], BF16, name="h_raw")
+        c_raw = keep.tile([P, TILES, HID], BF16, name="c_raw")
 
-        def load_x_pair(j):
-            nc.sync.dma_start(out=x_raw[:, 2 * j : 2 * j + 2, :], in_=x_rows[:, 2 * j : 2 * j + 2, :])
+        def load(raw, rows, j):
+            nc.sync.dma_start(out=raw[:, 2 * j : 2 * j + 2, :], in_=rows[:, 2 * j : 2 * j + 2, :])
 
-        load_x_pair(0)
-        load_x_pair(1)
+        def load_w(q):
+            nc.sync.dma_start(out=w_raw[:, q, :], in_=w_rows[q])
+
+        load(x_raw, x_rows, 0)
         nc.sync.dma_start(out=bias_rows[0:1, :], in_=bias_ih.unsqueeze(0))
         nc.sync.dma_start(out=bias_rows[1:2, :], in_=bias_hh.unsqueeze(0))
+        load_w(I_GATE)
+        load(h_raw, h_rows, 0)
         nc.sync.dma_start(out=w_codes[:].bitcast(I32), in_=w_ih_words[0].bitcast(I32))
         for quadrant in range(4):
             nc.sync.dma_start(
                 out=w_scales[32 * quadrant : 32 * quadrant + 4, :].bitcast(I32),
                 in_=w_ih_scales[0, 4 * quadrant : 4 * quadrant + 4, :].bitcast(I32),
             )
-        w_raw = keep.tile([P, GATES, ROWS * HID], BF16, name="w_raw")
-        h_raw = keep.tile([P, TILES, HID], BF16, name="h_raw")
-
-        def load_h_pair(j):
-            nc.sync.dma_start(out=h_raw[:, 2 * j : 2 * j + 2, :], in_=h_rows[:, 2 * j : 2 * j + 2, :])
-
-        for step, q in enumerate(GATE_ORDER):
-            nc.sync.dma_start(out=w_raw[:, q, :], in_=w_rows[q])
-            if step == 0:
-                load_h_pair(0)
-        for j in range(HEAD_PAIRS, PAIRS):
-            load_x_pair(j)
-        for j in range(1, PAIRS):
-            load_h_pair(j)
-        c_raw = keep.tile([P, TILES, HID], BF16, name="c_raw")
-        nc.sync.dma_start(out=c_raw[:], in_=c_rows)
+        load_w(G_GATE)
+        load_w(F_GATE)
+        load(x_raw, x_rows, 1)
+        load_w(O_GATE)
+        load(h_raw, h_rows, 1)
+        load(c_raw, c_rows, 0)
+        load(x_raw, x_rows, 2)
+        load(h_raw, h_rows, 2)
+        load(x_raw, x_rows, 3)
+        load(h_raw, h_rows, 3)
+        nc.sync.dma_start(out=c_raw[:, 2:, :], in_=c_rows[:, 2:, :])
 
         bias_sum = keep.tile([P, GATES, HID], F32, name="bias_sum")
         x_words = x_raw[:].bitcast(F32)
@@ -107,28 +121,29 @@ def tile_int8lstmcell_kernel(
         grouped_words = grouped[:].bitcast(F32).rearrange("p (t b u) -> p t b u", t=TILES, u=HALVES)
         x_codes = keep.tile([P, BATCH], U32, name="x_codes", align_bytes=64)
         x_scales = keep.tile([P, BATCH], U8, name="x_scales", align_bytes=64)
-
+        w_words = w_raw[:].bitcast(F32)
+        h_words = h_raw[:].bitcast(F32)
+        wT_words = keep.tile([P, HALVES, GATES, HID], F32, name="wT_words")
+        hT_words = keep.tile([P, HALVES, TILES, P], F32, name="hT_words")
         open_banks = {}
+
+        def new_bank():
+            return psum.tile([P, BANK], F32, name="bank")
+
+        def turn(out, in_):
+            nc.tensor.transpose(out=out, in_=in_, identity=ident[:])
 
         def turn_x_step(j, k):
             if k == 0:
-                open_banks["x", j] = psum.tile([P, BANK], F32, name="bank")
+                open_banks["x", j] = new_bank()
             planes = open_banks["x", j][:].rearrange("p (t u b) -> p t u b", t=2, u=HALVES)
             i, u = divmod(k, HALVES)
-            nc.tensor.transpose(
-                out=planes[:, i, u, :],
-                in_=x_words[:, 2 * j + i, u : IN // WORD : HALVES],
-                identity=ident[:],
-            )
+            turn(planes[:, i, u, :], x_words[:, 2 * j + i, u : IN // WORD : HALVES])
             if k == 2 * HALVES - 1:
                 nc.scalar.copy(
                     out=grouped_words[:, 2 * j : 2 * j + 2, :, :],
                     in_=planes.rearrange("p t u b -> p t b u"),
                 )
-
-        def turn_x_pair(j):
-            for k in range(2 * HALVES):
-                turn_x_step(j, k)
 
         def quantise_x_pair(j):
             rows = slice(2 * j * P, (2 * j + 2) * P)
@@ -138,23 +153,41 @@ def tile_int8lstmcell_kernel(
                 in_=grouped[:, 2 * j * IN : (2 * j + 2) * IN],
             )
 
+        def turn_h_step(j, k):
+            if k == 0:
+                open_banks["h", j] = new_bank()
+            planes = open_banks["h", j][:].rearrange("p (u t b) -> p u t b", u=HALVES, t=2)
+            u, i = divmod(k, 2)
+            turn(planes[:, u, i, :], h_words[:, 2 * j + i, u * P : (u + 1) * P])
+            if k == 2 * HALVES - 1:
+                nc.scalar.copy(out=hT_words[:, :, 2 * j : 2 * j + 2, :], in_=planes)
+
+        def turn_w_step(block, k, copy=nc.scalar.copy):
+            u, r = divmod(k, ROWS)
+            if r == 0:
+                open_banks["w", block] = new_bank()
+            bank = open_banks["w", block]
+            first = r * (HID // WORD) + u * P
+            turn(bank[:, r * P : (r + 1) * P], w_words[:, block, first : first + P])
+            if r == ROWS - 1:
+                copy(
+                    out=wT_words[:, u, block, :].rearrange("p (n r) -> p n r", r=ROWS),
+                    in_=bank[:].rearrange("p (r n) -> p n r", r=ROWS),
+                )
+
         def spread_bias(q):
-            bank = psum.tile([P, BANK], F32, name="bank")
+            bank = new_bank()
             nc.tensor.matmul(
                 out=bank[:], lhsT=ones[:], rhs=bias_rows[:, q * HID : (q + 1) * HID], start=True, stop=True
             )
-            nc.scalar.copy(out=bias_sum[:, q, :], in_=bank[:])
-
-        for j in range(HEAD_PAIRS):
-            turn_x_pair(j)
-            quantise_x_pair(j)
-            for q in GATE_ORDER[j * GATES // HEAD_PAIRS : (j + 1) * GATES // HEAD_PAIRS]:
-                spread_bias(q)
+            nc.vector.tensor_copy(out=bias_sum[:, q, :], in_=bank[:])
 
         gates = [states.tile([P, GATES, HID], F32, name="gates") for t in range(TILES)]
+        WHOLE = slice(0, HID)
+        SPLIT = [slice(0, HID // 2), slice(HID // 2, HID)]
 
-        def input_product(t, q):
-            bank = psum.tile([P, BANK], F32, name="bank")
+        def x_product(t, q):
+            bank = new_bank()
             nc.tensor.matmul_mx(
                 out=bank[:],
                 lhsT=x_codes[:, t * P : (t + 1) * P].bitcast(FP8X4),
@@ -166,137 +199,121 @@ def tile_int8lstmcell_kernel(
             )
             nc.vector.tensor_tensor(out=gates[t][:, q, :], in0=bank[:], in1=bias_sum[:, q, :], op=ADD)
 
-        w_words = w_raw[:].bitcast(F32)
-        h_words = h_raw[:].bitcast(F32)
-        wT_words = keep.tile([P, HALVES, GATES, HID], F32, name="wT_words")
-        hT_words = keep.tile([P, HALVES, TILES, P], F32, name="hT_words")
-
-        def turn_h_step(j, k):
-            if k == 0:
-                open_banks["h", j] = psum.tile([P, BANK], F32, name="bank")
-            planes = open_banks["h", j][:].rearrange("p (u t b) -> p u t b", u=HALVES, t=2)
-            u, i = divmod(k, 2)
-            nc.tensor.transpose(
-                out=planes[:, u, i, :],
-                in_=h_words[:, 2 * j + i, u * P : (u + 1) * P],
-                identity=ident[:],
-            )
-            if k == 2 * HALVES - 1:
-                nc.scalar.copy(out=hT_words[:, :, 2 * j : 2 * j + 2, :], in_=planes)
-
-        def turn_h_pair(j):
-            for k in range(2 * HALVES):
-                turn_h_step(j, k)
-
-        def turn_w_step(block, k):
-            u, r = divmod(k, ROWS)
-            if r == 0:
-                open_banks["w", block] = psum.tile([P, BANK], F32, name="bank")
-            bank = open_banks["w", block]
-            first = r * (HID // WORD) + u * P
-            nc.tensor.transpose(
-                out=bank[:, r * P : (r + 1) * P],
-                in_=w_words[:, block, first : first + P],
-                identity=ident[:],
-            )
-            if r == ROWS - 1:
-                nc.scalar.copy(
-                    out=wT_words[:, u, block, :].rearrange("p (n r) -> p n r", r=ROWS),
-                    in_=bank[:].rearrange("p (r n) -> p n r", r=ROWS),
-                )
-
-        for step in range(HEAD_LEAD):
-            for q in GATE_ORDER:
-                input_product(step, q)
-            if step == 0:
-                for k in range(HALVES * ROWS):
-                    turn_w_step(GATE_ORDER[0], k)
-                turn_h_pair(0)
-        woven = [(turn_w_step, block, k) for block in GATE_ORDER[1:] for k in range(HALVES * ROWS)]
-        DOUBLE = len(woven)
-        woven.extend([(turn_x_step, j, k) for j in range(HEAD_PAIRS, PAIRS) for k in range(2 * HALVES)])
-        woven.extend([(turn_h_step, j, k) for j in range(1, PAIRS) for k in range(2 * HALVES)])
-        woven_done = [0]
-
         wT = wT_words[:].bitcast(BF16).rearrange("p u q (n e) -> p u q n e", e=WORD)
         hT = hT_words[:].bitcast(BF16).rearrange("p u t (b e) -> p u t b e", e=WORD)
+        woven = []
+        woven.extend([(turn_w_step, G_GATE, k) for k in range(HALVES * ROWS)])
+        woven.extend([(turn_w_step, F_GATE, k) for k in range(HALVES * ROWS)])
+        woven.extend([(turn_w_step, O_GATE, k) for k in range(HALVES * ROWS)])
+        woven.extend([(turn_x_step, 1, k) for k in range(2 * HALVES)])
+        woven.extend([(turn_h_step, 1, k) for k in range(2 * HALVES)])
+        woven.extend([(turn_x_step, 2, k) for k in range(2 * HALVES)])
+        woven.extend([(turn_h_step, 2, k) for k in range(2 * HALVES)])
+        woven.extend([(turn_x_step, 3, k) for k in range(2 * HALVES)])
+        woven.extend([(turn_h_step, 3, k) for k in range(2 * HALVES)])
+        woven.reverse()
 
-        def gate(t, q):
-            if t == 0:
-                for late in range(HEAD_LEAD, LEAD):
-                    input_product(late, q)
-            if t + LEAD < TILES:
-                input_product(t + LEAD, q)
-            bank = psum.tile([P, BANK], F32, name="bank")
-            for u in range(HALVES):
-                for e in range(WORD):
-                    nc.tensor.matmul(
-                        out=bank[:],
-                        lhsT=hT[:, u, t, :, e],
-                        rhs=wT[:, u, q, :, e],
-                        start=(u == 0 and e == 0),
-                        stop=(u == HALVES - 1 and e == WORD - 1),
-                    )
-                    for again in range(2 if woven_done[0] < DOUBLE else 1):
-                        if woven_done[0] < len(woven):
-                            step, j, k = woven[woven_done[0]]
-                            woven_done[0] += 1
-                            step(j, k)
-            value = gates[t][:, q, :]
-            nc.vector.tensor_tensor(out=value, in0=bank[:], in1=value, op=ADD)
+        def weave(i, k):
+            for again in range(min(WEAVE[0 if i < HASTY else 1][k], len(woven))):
+                step, j, n = woven.pop()
+                step(j, n)
+
+        def h_product(i, cols=WHOLE):
+            t, q = UNITS[i]
+            bank = new_bank()
+            for k in range(HALVES * WORD):
+                u, e = divmod(k, WORD)
+                nc.tensor.matmul(
+                    out=bank[:, cols],
+                    lhsT=hT[:, u, t, :, e],
+                    rhs=wT[:, u, q, cols, e],
+                    start=(k == 0),
+                    stop=(k == HALVES * WORD - 1),
+                )
+                weave(i, k)
+            return bank
+
+        def finish(i, bank, cols=WHOLE):
+            t, q = UNITS[i]
+            value = gates[t][:, q, cols]
+            nc.vector.tensor_tensor(out=value, in0=bank[:, cols], in1=value, op=ADD)
+
+        def activate(i, cols=WHOLE):
+            t, q = UNITS[i]
+            value = gates[t][:, q, cols]
             nc.scalar.activation(out=value, in_=value, func=GATE_FUNC[q])
 
-        def input_term(t, engine):
-            i, g = gates[t][:, I_GATE, :], gates[t][:, G_GATE, :]
+        def input_term(t, engine, cols=WHOLE):
+            i, g = gates[t][:, I_GATE, cols], gates[t][:, G_GATE, cols]
             engine.tensor_tensor(out=i, in0=i, in1=g, op=MULT)
 
-        def forget_term(t, engine):
-            f = gates[t][:, F_GATE, :]
-            engine.tensor_tensor(out=f, in0=f, in1=c_raw[:, t, :], op=MULT)
+        def forget_term(t, engine, cols=WHOLE):
+            f = gates[t][:, F_GATE, cols]
+            engine.tensor_tensor(out=f, in0=f, in1=c_raw[:, t, cols], op=MULT)
 
-        def cell_state(t, engine):
-            i, f = gates[t][:, I_GATE, :], gates[t][:, F_GATE, :]
+        def cell_state(t, engine, cols=WHOLE):
+            i, f = gates[t][:, I_GATE, cols], gates[t][:, F_GATE, cols]
             engine.tensor_tensor(out=f, in0=i, in1=f, op=ADD)
-            nc.sync.dma_start(out=c_out[:, t, :], in_=f)
+            nc.sync.dma_start(out=c_out[:, t, cols], in_=f)
 
-        def cell_tanh(t):
-            nc.scalar.activation(out=gates[t][:, G_GATE, :], in_=gates[t][:, F_GATE, :], func=TANH)
+        def cell_tanh(t, cols=WHOLE):
+            nc.scalar.activation(out=gates[t][:, G_GATE, cols], in_=gates[t][:, F_GATE, cols], func=TANH)
 
-        def hidden_state(t, engine):
-            g, o = gates[t][:, G_GATE, :], gates[t][:, O_GATE, :]
+        def hidden_state(t, engine, cols=WHOLE):
+            g, o = gates[t][:, G_GATE, cols], gates[t][:, O_GATE, cols]
             engine.tensor_tensor(out=o, in0=o, in1=g, op=MULT)
-            nc.sync.dma_start(out=h_out[:, t, :], in_=o)
+            nc.sync.dma_start(out=h_out[:, t, cols], in_=o)
 
-        LAST = TILES - 1
+        for k in range(2 * HALVES):
+            turn_x_step(0, k)
+        quantise_x_pair(0)
+        spread_bias(I_GATE)
+        spread_bias(G_GATE)
+        for k in range(HALVES * ROWS):
+            turn_w_step(I_GATE, k)
+        spread_bias(F_GATE)
+        for k in range(2 * HALVES):
+            turn_h_step(0, k)
+        spread_bias(O_GATE)
+
+        steps = {}
+
+        def behind(t, q, late, step, *which):
+            steps.setdefault(UNITS.index((t, q)) + late, []).append((step, *which))
+
         for t in range(TILES):
-            busy = t < LAST
-            was_busy = True
-            if t != 1:
-                gate(t, I_GATE)
-            if t == 0:
-                gate(1, I_GATE)
-            gate(t, G_GATE)
-            if not was_busy:
-                cell_state(t - 1, nc.vector)
-                cell_tanh(t - 1)
-            gate(t, F_GATE)
-            input_term(t, nc.vector if t == LAST else nc.gpsimd)
-            if t > 0 and was_busy:
-                cell_tanh(t - 1)
+            behind(t, G_GATE, 0, input_term, t, nc.gpsimd)
             if t < LAST - 1:
-                gate(t, O_GATE)
-            if t == LAST:
-                gate(t - 1, O_GATE)
-            if t == 0:
-                for j in range(HEAD_PAIRS, PAIRS):
-                    quantise_x_pair(j)
-            forget_term(t, nc.vector if t == LAST else nc.gpsimd)
-            if busy:
-                cell_state(t, nc.gpsimd)
-            if t == LAST:
-                gate(t, O_GATE)
-                cell_state(t, nc.vector)
-            if t > 0:
-                hidden_state(t - 1, nc.gpsimd if busy else nc.vector)
-        cell_tanh(LAST)
-        hidden_state(LAST, nc.vector)
+                behind(t, F_GATE, 0, forget_term, t, nc.gpsimd)
+                behind(t, F_GATE, 0, cell_state, t, nc.gpsimd)
+                behind(t, F_GATE, TANH_BEHIND, cell_tanh, t)
+            if t < LAST - 2:
+                behind(t, F_GATE, TANH_BEHIND + 1, hidden_state, t, nc.gpsimd)
+        behind(LAST - 1, F_GATE, 1, forget_term, LAST - 1, nc.vector)
+        behind(LAST - 1, F_GATE, 2, cell_state, LAST - 1, nc.vector)
+        behind(LAST, F_GATE, 0, cell_tanh, LAST - 1)
+        behind(LAST - 2, O_GATE, 0, forget_term, LAST, nc.vector)
+        behind(LAST - 1, O_GATE, 0, cell_state, LAST, nc.vector)
+        behind(LAST - 1, O_GATE, 0, cell_tanh, LAST)
+        behind(LAST - 1, O_GATE, 0, hidden_state, LAST - 2, nc.gpsimd)
+
+        x_done = 0
+        for i in range(len(UNITS) - 1):
+            while x_done < x_products_before(i):
+                x_product(*UNITS[x_done])
+                x_done += 1
+            bank = h_product(i)
+            finish(i, bank)
+            activate(i)
+            if i in QUANTISE_BEHIND:
+                quantise_x_pair(QUANTISE_BEHIND[i])
+            for step, *which in steps.get(i, []):
+                step(*which)
+        i = len(UNITS) - 1
+        banks = [h_product(i, cols) for cols in SPLIT]
+        for bank, cols in zip(banks, SPLIT):
+            finish(i, bank, cols)
+            activate(i, cols)
+        hidden_state(LAST - 1, nc.vector)
+        for cols in SPLIT:
+            hidden_state(LAST, nc.vector, cols)

@@ -40,7 +40,7 @@ UNITS = (
 
 
 def x_products_before(i):
-    return min(3 + 5 * i // 4, i + 8, len(UNITS))
+    return min(3 + i, len(UNITS))
 
 
 WEAVE = ((2, 2, 2, 2), (1, 1, 1, 1))
@@ -289,8 +289,8 @@ def tile_int8lstmcell_kernel(
                 behind(t, F_GATE, TANH_BEHIND, cell_tanh, t)
             if t < LAST - 2:
                 behind(t, F_GATE, TANH_BEHIND + 1, hidden_state, t, nc.gpsimd)
-        behind(LAST - 1, F_GATE, 1, forget_term, LAST - 1, nc.vector)
-        behind(LAST - 1, F_GATE, 2, cell_state, LAST - 1, nc.vector)
+        behind(LAST - 1, F_GATE, 0, forget_term, LAST - 1, nc.gpsimd)
+        behind(LAST - 1, F_GATE, 0, cell_state, LAST - 1, nc.gpsimd)
         behind(LAST, F_GATE, 0, cell_tanh, LAST - 1)
         behind(LAST - 2, O_GATE, 0, forget_term, LAST, nc.vector)
         behind(LAST - 1, O_GATE, 0, cell_state, LAST, nc.vector)

@@ -72,7 +72,7 @@ def tile_int8lstmcell_kernel(
         nc.vector.memset(bias_rows[:].bitcast(I32), 0)
         ones = keep.tile([P, P], BF16, name="ones")
         nc.vector.memset(ones[:], 1.0)
-        w_scales = keep.tile([P, GATES * HID], U8, name="w_scales", align_bytes=64)
+        w_scales = keep.tile([P, GATES * HID], U8, name="w_scales", align_bytes=256)
         nc.vector.memset(w_scales[:].bitcast(I32), 0)
         ident = keep.tile([P, P], F32, name="ident")
         make_identity(nc, ident[:])
@@ -81,7 +81,7 @@ def tile_int8lstmcell_kernel(
         nc.scalar.activation(out=warm[:], in_=warm[:], func=SIGMOID)
 
         x_raw = keep.tile([P, TILES, IN], BF16, name="x_raw")
-        w_codes = keep.tile([P, 2 * GATES * HID], U8, name="w_codes", align_bytes=64)
+        w_codes = keep.tile([P, 2 * GATES * HID], U8, name="w_codes", align_bytes=256)
         w_raw = keep.tile([P, GATES, ROWS * HID], BF16, name="w_raw")
         h_raw = keep.tile([P, TILES, HID], BF16, name="h_raw")
         c_raw = keep.tile([P, TILES, HID], BF16, name="c_raw")
@@ -119,8 +119,8 @@ def tile_int8lstmcell_kernel(
         x_words = x_raw[:].bitcast(F32)
         grouped = keep.tile([P, TILES * IN], BF16, name="grouped", align_bytes=64)
         grouped_words = grouped[:].bitcast(F32).rearrange("p (t b u) -> p t b u", t=TILES, u=HALVES)
-        x_codes = keep.tile([P, BATCH], U32, name="x_codes", align_bytes=64)
-        x_scales = keep.tile([P, BATCH], U8, name="x_scales", align_bytes=64)
+        x_codes = keep.tile([P, BATCH], U32, name="x_codes", align_bytes=256)
+        x_scales = keep.tile([P, BATCH], U8, name="x_scales", align_bytes=256)
         w_words = w_raw[:].bitcast(F32)
         h_words = h_raw[:].bitcast(F32)
         wT_words = keep.tile([P, HALVES, GATES, HID], F32, name="wT_words")

@@ -33,14 +33,14 @@ GATE_FUNC = (SIGMOID, SIGMOID, TANH, SIGMOID)
 LAST = TILES - 1
 UNITS = (
     [(0, I_GATE), (1, I_GATE), (0, G_GATE), (0, F_GATE), (0, O_GATE), (1, G_GATE), (1, F_GATE), (1, O_GATE)]
-    + [(t, q) for t in range(2, LAST - 2) for q in GATE_ORDER]
-    + [(t, q) for t in (LAST - 2, LAST - 1, LAST) for q in GATE_ORDER[:3]]
-    + [(t, O_GATE) for t in (LAST - 2, LAST - 1, LAST)]
+    + [(t, q) for t in range(2, TILES - 4) for q in GATE_ORDER]
+    + [(t, q) for t in range(TILES - 4, TILES) for q in GATE_ORDER[:3]]
+    + [(t, O_GATE) for t in range(TILES - 4, TILES)]
 )
 
 
 def x_products_before(i):
-    return min(3 + i, len(UNITS))
+    return min(i + (3 if i < 8 else 4), len(UNITS))
 
 
 WEAVE = ((2, 2, 2, 2), (1, 1, 1, 1))
@@ -282,20 +282,23 @@ def tile_int8lstmcell_kernel(
             steps.setdefault(UNITS.index((t, q)) + late, []).append((step, *which))
 
         for t in range(TILES):
-            behind(t, G_GATE, 0, input_term, t, nc.gpsimd)
+            if t < LAST:
+                behind(t, G_GATE, 0, input_term, t, nc.gpsimd)
             if t < LAST - 1:
                 behind(t, F_GATE, 0, forget_term, t, nc.gpsimd)
                 behind(t, F_GATE, 0, cell_state, t, nc.gpsimd)
                 behind(t, F_GATE, TANH_BEHIND, cell_tanh, t)
-            if t < LAST - 2:
+            if t < TILES - 4:
                 behind(t, F_GATE, TANH_BEHIND + 1, hidden_state, t, nc.gpsimd)
         behind(LAST - 1, F_GATE, 0, forget_term, LAST - 1, nc.gpsimd)
         behind(LAST - 1, F_GATE, 0, cell_state, LAST - 1, nc.gpsimd)
+        behind(LAST, G_GATE, 0, input_term, LAST, nc.gpsimd)
         behind(LAST, F_GATE, 0, cell_tanh, LAST - 1)
-        behind(LAST - 2, O_GATE, 0, forget_term, LAST, nc.vector)
-        behind(LAST - 1, O_GATE, 0, cell_state, LAST, nc.vector)
-        behind(LAST - 1, O_GATE, 0, cell_tanh, LAST)
-        behind(LAST - 1, O_GATE, 0, hidden_state, LAST - 2, nc.gpsimd)
+        behind(LAST, F_GATE, 1, forget_term, LAST, nc.vector)
+        behind(LAST, F_GATE, 2, cell_state, LAST, nc.vector)
+        behind(LAST, F_GATE, 2, cell_tanh, LAST)
+        behind(LAST - 3, O_GATE, 0, hidden_state, LAST - 3, nc.gpsimd)
+        behind(LAST - 2, O_GATE, 0, hidden_state, LAST - 2, nc.gpsimd)
 
         x_done = 0
         for i in range(len(UNITS) - 1):

@@ -16,6 +16,7 @@ SIGMOID = mybir.ActivationFunctionType.Sigmoid
 TANH = mybir.ActivationFunctionType.Tanh
 
 P = 128
+QUADRANT = 32
 BATCH, IN, HID = 1024, 512, 512
 GATES = 4
 TILES = BATCH // P
@@ -68,14 +69,16 @@ def tile_int8lstmcell_kernel(
         c_out = out_1.rearrange("(p t) n -> p t n", t=TILES)
         w_rows = w_hh.rearrange("(q p r) k -> q p (r k)", q=GATES, r=ROWS)
 
-        bias_rows = keep.tile([P, GATES * HID], BF16, name="bias_rows")
+        bias_rows = keep.tile([P, HID], BF16, name="bias_rows")
         nc.vector.memset(bias_rows[:].bitcast(I32), 0)
-        ones = keep.tile([P, P], BF16, name="ones")
-        nc.vector.memset(ones[:], 1.0)
         w_scales = keep.tile([P, GATES * HID], U8, name="w_scales", align_bytes=256)
         nc.vector.memset(w_scales[:].bitcast(I32), 0)
         ident = keep.tile([P, P], F32, name="ident")
         make_identity(nc, ident[:])
+        pick = keep.tile([P, GATES, P], BF16, name="pick")
+        nc.gpsimd.memset(pick[:], 0.0)
+        for q in range(GATES):
+            nc.gpsimd.memset(pick[QUADRANT * q : QUADRANT * (q + 1), q, :], 1.0)
         warm = keep.tile([P, 1], F32, name="warm")
         nc.vector.memset(warm[:], 0.0)
         nc.scalar.activation(out=warm[:], in_=warm[:], func=SIGMOID)
@@ -93,8 +96,8 @@ def tile_int8lstmcell_kernel(
             nc.sync.dma_start(out=w_raw[:, q, :], in_=w_rows[q])
 
         load(x_raw, x_rows, 0)
-        nc.sync.dma_start(out=bias_rows[0:1, :], in_=bias_ih.unsqueeze(0))
-        nc.sync.dma_start(out=bias_rows[1:2, :], in_=bias_hh.unsqueeze(0))
+        for row, bias in enumerate((bias_ih, bias_hh)):
+            nc.sync.dma_start(out=bias_rows[row:P:QUADRANT, :], in_=bias.rearrange("(q n) -> q n", q=GATES))
         load_w(I_GATE)
         load(h_raw, h_rows, 0)
         nc.sync.dma_start(out=w_codes[:].bitcast(I32), in_=w_ih_words[0].bitcast(I32))
@@ -178,9 +181,10 @@ def tile_int8lstmcell_kernel(
         def spread_bias(q):
             bank = new_bank()
             nc.tensor.matmul(
-                out=bank[:], lhsT=ones[:], rhs=bias_rows[:, q * HID : (q + 1) * HID], start=True, stop=True
+                out=bank[:], lhsT=pick[:, q, :], rhs=bias_rows[:], start=True, stop=True
             )
-            nc.vector.tensor_copy(out=bias_sum[:, q, :], in_=bank[:])
+            copy = nc.vector.tensor_copy if q in GATE_ORDER[:2] else nc.scalar.copy
+            copy(out=bias_sum[:, q, :], in_=bank[:])
 
         gates = [states.tile([P, GATES, HID], F32, name="gates") for t in range(TILES)]
         WHOLE = slice(0, HID)
@@ -270,10 +274,10 @@ def tile_int8lstmcell_kernel(
         spread_bias(I_GATE)
         spread_bias(G_GATE)
         for k in range(HALVES * ROWS):
-            turn_w_step(I_GATE, k)
-        spread_bias(F_GATE)
+            turn_w_step(I_GATE, k, nc.scalar.copy if k < ROWS else nc.vector.tensor_copy)
         for k in range(2 * HALVES):
             turn_h_step(0, k)
+        spread_bias(F_GATE)
         spread_bias(O_GATE)
 
         steps = {}

from contextlib import ExitStack

import concourse.mybir as mybir
from concourse.masks import make_identity

F32 = mybir.dt.float32
BF16 = mybir.dt.bfloat16
I32 = mybir.dt.int32
U32 = mybir.dt.uint32
U8 = mybir.dt.uint8
FP8X4 = mybir.dt.float8_e4m3fn_x4
FP4X4 = mybir.dt.float4_e2m1fn_x4
ADD = mybir.AluOpType.add
MULT = mybir.AluOpType.mult
SIGMOID = mybir.ActivationFunctionType.Sigmoid
TANH = mybir.ActivationFunctionType.Tanh

P = 128
QUADRANT = 32
BATCH, IN, HID = 1024, 512, 512
GATES = 4
TILES = BATCH // P
PAIRS = TILES // 2
BANK = 512
PSUM_BANKS = 8
HALVES = 2
WORD = 2
ROWS = HID // P

I_GATE, F_GATE, G_GATE, O_GATE = 0, 1, 2, 3
GATE_ORDER = (I_GATE, G_GATE, F_GATE, O_GATE)
GATE_FUNC = (SIGMOID, SIGMOID, TANH, SIGMOID)

LAST = TILES - 1
UNITS = (
    [(0, I_GATE), (1, I_GATE), (0, G_GATE), (0, F_GATE), (0, O_GATE), (1, G_GATE), (1, F_GATE), (1, O_GATE)]
    + [(t, q) for t in range(2, TILES - 4) for q in GATE_ORDER]
    + [(t, q) for t in range(TILES - 4, TILES) for q in GATE_ORDER[:3]]
    + [(t, O_GATE) for t in range(TILES - 4, TILES)]
)


def x_products_before(i):
    return min(i + (3 if i < 8 else 4), len(UNITS))


WEAVE = ((2, 2, 2, 2), (1, 1, 1, 1))
HASTY = 3
QUANTISE_BEHIND = {3: 1, 8: 2, 12: 3}
TANH_BEHIND = 4

FLOPS = 2 * BATCH * GATES * HID * (IN + HID)


def tile_int8lstmcell_kernel(
    tc, x, h_prev, c_prev, w_ih_words, w_ih_scales, w_hh, bias_ih, bias_hh, out_0, out_1
):
    nc = tc.nc
    with ExitStack() as ctx:
        ctx.enter_context(tc.manual_schedule())
        keep = ctx.enter_context(tc.tile_pool(name="keep", bufs=1))
        states = ctx.enter_context(tc.tile_pool(name="states", bufs=TILES))
        psum = ctx.enter_context(tc.psum_pool(name="psum", bufs=PSUM_BANKS))

        x_rows = x.rearrange("(p t) k -> p t k", t=TILES)
        h_rows = h_prev.rearrange("(p t) k -> p t k", t=TILES)
        c_rows = c_prev.rearrange("(p t) n -> p t n", t=TILES)
        h_out = out_0.rearrange("(p t) n -> p t n", t=TILES)
        c_out = out_1.rearrange("(p t) n -> p t n", t=TILES)
        w_rows = w_hh.rearrange("(q p r) k -> q p (r k)", q=GATES, r=ROWS)

        bias_rows = keep.tile([P, HID], BF16, name="bias_rows")
        nc.vector.memset(bias_rows[:].bitcast(I32), 0)
        w_scales = keep.tile([P, GATES * HID], U8, name="w_scales", align_bytes=256)
        nc.vector.memset(w_scales[:].bitcast(I32), 0)
        ident = keep.tile([P, P], F32, name="ident")
        make_identity(nc, ident[:])
        pick = keep.tile([P, GATES, P], BF16, name="pick")
        nc.gpsimd.memset(pick[:], 0.0)
        for q in range(GATES):
            nc.gpsimd.memset(pick[QUADRANT * q : QUADRANT * (q + 1), q, :], 1.0)
        warm = keep.tile([P, 1], F32, name="warm")
        nc.vector.memset(warm[:], 0.0)
        nc.scalar.activation(out=warm[:], in_=warm[:], func=SIGMOID)

        x_raw = keep.tile([P, TILES, IN], BF16, name="x_raw")
        w_codes = keep.tile([P, 2 * GATES * HID], U8, name="w_codes", align_bytes=256)
        w_raw = keep.tile([P, GATES, ROWS * HID], BF16, name="w_raw")
        h_raw = keep.tile([P, TILES, HID], BF16, name="h_raw")
        c_raw = keep.tile([P, TILES, HID], BF16, name="c_raw")

        def load(raw, rows, j):
            nc.sync.dma_start(out=raw[:, 2 * j : 2 * j + 2, :], in_=rows[:, 2 * j : 2 * j + 2, :])

        def load_w(q):
            nc.sync.dma_start(out=w_raw[:, q, :], in_=w_rows[q])

        load(x_raw, x_rows, 0)
        for row, bias in enumerate((bias_ih, bias_hh)):
            nc.sync.dma_start(out=bias_rows[row:P:QUADRANT, :], in_=bias.rearrange("(q n) -> q n", q=GATES))
        load_w(I_GATE)
        load(h_raw, h_rows, 0)
        nc.sync.dma_start(out=w_codes[:].bitcast(I32), in_=w_ih_words[0].bitcast(I32))
        for quadrant in range(4):
            nc.sync.dma_start(
                out=w_scales[32 * quadrant : 32 * quadrant + 4, :].bitcast(I32),
                in_=w_ih_scales[0, 4 * quadrant : 4 * quadrant + 4, :].bitcast(I32),
            )
        load_w(G_GATE)
        load_w(F_GATE)
        load(x_raw, x_rows, 1)
        load_w(O_GATE)
        load(h_raw, h_rows, 1)
        load(c_raw, c_rows, 0)
        load(x_raw, x_rows, 2)
        load(h_raw, h_rows, 2)
        load(x_raw, x_rows, 3)
        load(h_raw, h_rows, 3)
        nc.sync.dma_start(out=c_raw[:, 2:, :], in_=c_rows[:, 2:, :])

        bias_sum = keep.tile([P, GATES, HID], F32, name="bias_sum")
        x_words = x_raw[:].bitcast(F32)
        grouped = keep.tile([P, TILES * IN], BF16, name="grouped", align_bytes=64)
        grouped_words = grouped[:].bitcast(F32).rearrange("p (t b u) -> p t b u", t=TILES, u=HALVES)
        x_codes = keep.tile([P, BATCH], U32, name="x_codes", align_bytes=256)
        x_scales = keep.tile([P, BATCH], U8, name="x_scales", align_bytes=256)
        w_words = w_raw[:].bitcast(F32)
        h_words = h_raw[:].bitcast(F32)
        wT_words = keep.tile([P, HALVES, GATES, HID], F32, name="wT_words")
        hT_words = keep.tile([P, HALVES, TILES, P], F32, name="hT_words")
        open_banks = {}

        def new_bank():
            return psum.tile([P, BANK], F32, name="bank")

        def turn(out, in_):
            nc.tensor.transpose(out=out, in_=in_, identity=ident[:])

        def turn_x_step(j, k):
            if k == 0:
                open_banks["x", j] = new_bank()
            planes = open_banks["x", j][:].rearrange("p (t u b) -> p t u b", t=2, u=HALVES)
            i, u = divmod(k, HALVES)
            turn(planes[:, i, u, :], x_words[:, 2 * j + i, u : IN // WORD : HALVES])
            if k == 2 * HALVES - 1:
                nc.scalar.copy(
                    out=grouped_words[:, 2 * j : 2 * j + 2, :, :],
                    in_=planes.rearrange("p t u b -> p t b u"),
                )

        def quantise_x_pair(j):
            rows = slice(2 * j * P, (2 * j + 2) * P)
            nc.vector.quantize_mx(
                out=x_codes[:, rows].bitcast(FP8X4),
                scales=x_scales[:, rows],
                in_=grouped[:, 2 * j * IN : (2 * j + 2) * IN],
            )

        def turn_h_step(j, k):
            if k == 0:
                open_banks["h", j] = new_bank()
            planes = open_banks["h", j][:].rearrange("p (u t b) -> p u t b", u=HALVES, t=2)
            u, i = divmod(k, 2)
            turn(planes[:, u, i, :], h_words[:, 2 * j + i, u * P : (u + 1) * P])
            if k == 2 * HALVES - 1:
                nc.scalar.copy(out=hT_words[:, :, 2 * j : 2 * j + 2, :], in_=planes)

        def turn_w_step(block, k, copy=nc.scalar.copy):
            u, r = divmod(k, ROWS)
            if r == 0:
                open_banks["w", block] = new_bank()
            bank = open_banks["w", block]
            first = r * (HID // WORD) + u * P
            turn(bank[:, r * P : (r + 1) * P], w_words[:, block, first : first + P])
            if r == ROWS - 1:
                copy(
                    out=wT_words[:, u, block, :].rearrange("p (n r) -> p n r", r=ROWS),
                    in_=bank[:].rearrange("p (r n) -> p n r", r=ROWS),
                )

        def spread_bias(q):
            bank = new_bank()
            nc.tensor.matmul(
                out=bank[:], lhsT=pick[:, q, :], rhs=bias_rows[:], start=True, stop=True
            )
            copy = nc.vector.tensor_copy if q in GATE_ORDER[:2] else nc.scalar.copy
            copy(out=bias_sum[:, q, :], in_=bank[:])

        gates = [states.tile([P, GATES, HID], F32, name="gates") for t in range(TILES)]
        WHOLE = slice(0, HID)
        SPLIT = [slice(0, HID // 2), slice(HID // 2, HID)]

        def x_product(t, q):
            bank = new_bank()
            nc.tensor.matmul_mx(
                out=bank[:],
                lhsT=x_codes[:, t * P : (t + 1) * P].bitcast(FP8X4),
                lhsT_scale=x_scales[:, t * P : (t + 1) * P],
                rhs=w_codes[:, 2 * q * HID : 2 * (q + 1) * HID].bitcast(FP4X4),
                rhs_scale=w_scales[:, q * HID : (q + 1) * HID],
                start=True,
                stop=True,
            )
            nc.vector.tensor_tensor(out=gates[t][:, q, :], in0=bank[:], in1=bias_sum[:, q, :], op=ADD)

        wT = wT_words[:].bitcast(BF16).rearrange("p u q (n e) -> p u q n e", e=WORD)
        hT = hT_words[:].bitcast(BF16).rearrange("p u t (b e) -> p u t b e", e=WORD)
        woven = []
        woven.extend([(turn_w_step, G_GATE, k) for k in range(HALVES * ROWS)])
        woven.extend([(turn_w_step, F_GATE, k) for k in range(HALVES * ROWS)])
        woven.extend([(turn_w_step, O_GATE, k) for k in range(HALVES * ROWS)])
        woven.extend([(turn_x_step, 1, k) for k in range(2 * HALVES)])
        woven.extend([(turn_h_step, 1, k) for k in range(2 * HALVES)])
        woven.extend([(turn_x_step, 2, k) for k in range(2 * HALVES)])
        woven.extend([(turn_h_step, 2, k) for k in range(2 * HALVES)])
        woven.extend([(turn_x_step, 3, k) for k in range(2 * HALVES)])
        woven.extend([(turn_h_step, 3, k) for k in range(2 * HALVES)])
        woven.reverse()

        def weave(i, k):
            for again in range(min(WEAVE[0 if i < HASTY else 1][k], len(woven))):
                step, j, n = woven.pop()
                step(j, n)

        def h_product(i, cols=WHOLE):
            t, q = UNITS[i]
            bank = new_bank()
            for k in range(HALVES * WORD):
                u, e = divmod(k, WORD)
                nc.tensor.matmul(
                    out=bank[:, cols],
                    lhsT=hT[:, u, t, :, e],
                    rhs=wT[:, u, q, cols, e],
                    start=(k == 0),
                    stop=(k == HALVES * WORD - 1),
                )
                weave(i, k)
            return bank

        def finish(i, bank, cols=WHOLE):
            t, q = UNITS[i]
            value = gates[t][:, q, cols]
            nc.vector.tensor_tensor(out=value, in0=bank[:, cols], in1=value, op=ADD)

        def activate(i, cols=WHOLE):
            t, q = UNITS[i]
            value = gates[t][:, q, cols]
            nc.scalar.activation(out=value, in_=value, func=GATE_FUNC[q])

        def input_term(t, engine, cols=WHOLE):
            i, g = gates[t][:, I_GATE, cols], gates[t][:, G_GATE, cols]
            engine.tensor_tensor(out=i, in0=i, in1=g, op=MULT)

        def forget_term(t, engine, cols=WHOLE):
            f = gates[t][:, F_GATE, cols]
            engine.tensor_tensor(out=f, in0=f, in1=c_raw[:, t, cols], op=MULT)

        def cell_state(t, engine, cols=WHOLE):
            i, f = gates[t][:, I_GATE, cols], gates[t][:, F_GATE, cols]
            engine.tensor_tensor(out=f, in0=i, in1=f, op=ADD)
            nc.sync.dma_start(out=c_out[:, t, cols], in_=f)

        def cell_tanh(t, cols=WHOLE):
            nc.scalar.activation(out=gates[t][:, G_GATE, cols], in_=gates[t][:, F_GATE, cols], func=TANH)

        def hidden_state(t, engine, cols=WHOLE):
            g, o = gates[t][:, G_GATE, cols], gates[t][:, O_GATE, cols]
            engine.tensor_tensor(out=o, in0=o, in1=g, op=MULT)
            nc.sync.dma_start(out=h_out[:, t, cols], in_=o)

        for k in range(2 * HALVES):
            turn_x_step(0, k)
        quantise_x_pair(0)
        spread_bias(I_GATE)
        spread_bias(G_GATE)
        for k in range(HALVES * ROWS):
            turn_w_step(I_GATE, k, nc.scalar.copy if k < ROWS else nc.vector.tensor_copy)
        for k in range(2 * HALVES):
            turn_h_step(0, k)
        spread_bias(F_GATE)
        spread_bias(O_GATE)

        steps = {}

        def behind(t, q, late, step, *which):
            steps.setdefault(UNITS.index((t, q)) + late, []).append((step, *which))

        for t in range(TILES):
            if t < LAST:
                behind(t, G_GATE, 0, input_term, t, nc.gpsimd)
            if t < LAST - 1:
                behind(t, F_GATE, 0, forget_term, t, nc.gpsimd)
                behind(t, F_GATE, 0, cell_state, t, nc.gpsimd)
                behind(t, F_GATE, TANH_BEHIND, cell_tanh, t)
            if t < TILES - 4:
                behind(t, F_GATE, TANH_BEHIND + 1, hidden_state, t, nc.gpsimd)
        behind(LAST - 1, F_GATE, 0, forget_term, LAST - 1, nc.gpsimd)
        behind(LAST - 1, F_GATE, 0, cell_state, LAST - 1, nc.gpsimd)
        behind(LAST, G_GATE, 0, input_term, LAST, nc.gpsimd)
        behind(LAST, F_GATE, 0, cell_tanh, LAST - 1)
        behind(LAST, F_GATE, 1, forget_term, LAST, nc.vector)
        behind(LAST, F_GATE, 2, cell_state, LAST, nc.vector)
        behind(LAST, F_GATE, 2, cell_tanh, LAST)
        behind(LAST - 3, O_GATE, 0, hidden_state, LAST - 3, nc.gpsimd)
        behind(LAST - 2, O_GATE, 0, hidden_state, LAST - 2, nc.gpsimd)

        x_done = 0
        for i in range(len(UNITS) - 1):
            while x_done < x_products_before(i):
                x_product(*UNITS[x_done])
                x_done += 1
            bank = h_product(i)
            finish(i, bank)
            activate(i)
            if i in QUANTISE_BEHIND:
                quantise_x_pair(QUANTISE_BEHIND[i])
            for step, *which in steps.get(i, []):
                step(*which)
        i = len(UNITS) - 1
        banks = [h_product(i, cols) for cols in SPLIT]
        for bank, cols in zip(banks, SPLIT):
            finish(i, bank, cols)
            activate(i, cols)
        hidden_state(LAST - 1, nc.vector)
        for cols in SPLIT:
            hidden_state(LAST, nc.vector, cols)
